import numpy as np
import ml_dtypes


def mxq(x, axis, fmt="e4m3"):
    dtype, down = {"e4m3": (ml_dtypes.float8_e4m3fn, 7), "e5m2": (ml_dtypes.float8_e5m2, 14)}[fmt]
    v = np.moveaxis(np.asarray(x, np.float32).astype(ml_dtypes.bfloat16).astype(np.float64), axis, -1)
    blocks = v.reshape(v.shape[:-1] + (-1, 32))
    amax = np.abs(blocks).max(-1, keepdims=True)
    byte = np.maximum(np.where(amax > 0, np.frexp(amax)[1] - 1 + 127, 0) - down, 1)
    scale = np.exp2(byte - 127.0)
    codes = (blocks / scale).astype(np.float32).astype(dtype).astype(np.float64)
    return np.moveaxis((codes * scale).reshape(v.shape), -1, axis)


WIDE = False


def mx_kscale(k):
    if not WIDE:
        return np.ones(k)
    levels = np.array([10, -10, 5, -5, 0])
    a = np.random.permutation(np.resize(levels, k // 512 * 4)).reshape(k // 512, 4)
    idx = np.arange(k)
    return np.exp2(a[idx // 512, idx % 128 // 32])


BF16 = ml_dtypes.bfloat16


def bf(x):
    return np.asarray(x, np.float32).astype(BF16)


def f64(x):
    return np.asarray(x).astype(np.float64)


E2M1 = np.array([0.0, 0.5, 1.0, 1.5, 2.0, 3.0, 4.0, 6.0, -0.0, -0.5, -1.0, -1.5, -2.0, -3.0, -4.0, -6.0])


def pack_weight(w, fmt):
    k, n = w.shape
    w = f64(bf(w)).reshape(k // 32, 32, n)
    amax = np.abs(w).max(1)
    if fmt == "e4m3":
        byte = np.frexp(amax)[1] - 1 + 127 - 7
    else:
        mant, ex = np.frexp(amax / 6.0)
        byte = np.where(mant > 0.5, ex, ex - 1) + 127
    byte = np.clip(np.where(amax > 0, byte, 1), 1, 254)
    scaled = (w * np.exp2(127.0 - byte)[:, None, :]).reshape(k, n).astype(np.float32)
    by_word = np.ascontiguousarray(scaled.reshape(k // 512, 128, 4, n).transpose(0, 1, 3, 2))
    if fmt == "e4m3":
        words = by_word.astype(ml_dtypes.float8_e4m3fn).view(np.uint8)
    else:
        c = by_word.astype(ml_dtypes.float4_e2m1fn).view(np.uint8) & 0xF
        words = c[..., 0::2] | (c[..., 1::2] << 4)
    return np.ascontiguousarray(words), np.ascontiguousarray(byte.astype(np.uint8).reshape(k // 512, 16, n))


def unpack_weight(words, scales, fmt):
    g, p, n, _ = words.shape
    if fmt == "e4m3":
        vals = np.ascontiguousarray(words).view(ml_dtypes.float8_e4m3fn).astype(np.float64)
    else:
        nib = np.empty((g, p, n, 4), np.uint8)
        nib[..., 0::2] = words & 0xF
        nib[..., 1::2] = words >> 4
        vals = E2M1[nib]
    vals = vals * np.repeat(np.exp2(scales.astype(np.float64) - 127.0), 8, axis=1)[..., None]
    return vals.transpose(0, 1, 3, 2).reshape(g * 512, n)


N, D, C, M = 128, 2048, 64, 64
LAMDA = 0.00390625
VS = 1.0 / (LAMDA * D)


def setup_inputs():
    s = mx_kscale(D)
    x = bf(np.random.standard_normal((N, D)) * s)
    x_var = bf(np.random.uniform(0.0, 1.0, (N, D)) * (0.5 + np.random.uniform(0.0, 1.0, (N, 1))) * 2.0 * VS)
    pm = np.random.standard_normal((C, M, D)) / np.sqrt(D) / s
    cat = np.ascontiguousarray(pm.swapaxes(1, 2)).reshape(-1, M)
    words, scales = pack_weight(cat, "e4m3")
    proto_var = bf(np.random.uniform(0.0, 1.0, (C, M, D)) * (0.5 + np.random.uniform(0.0, 1.0, (C, M, 1))) * 2.0 * VS)
    return {"x": x,
            "x_var": x_var,
            "proto_mean_words": words,
            "proto_mean_scales": scales,
            "proto_var": proto_var}


def reference(x, x_var, proto_mean_words, proto_mean_scales, proto_var):
    xv, pv = f64(x_var), f64(proto_var)
    dot = (mxq(f64(x), 1, "e4m3") @ unpack_weight(proto_mean_words, proto_mean_scales, "e4m3").reshape(C, D, M).swapaxes(1, 2).reshape(C * M, D).T).reshape(N, C, M)
    cross = (mxq(np.sqrt(xv), 1, "e4m3") @ mxq(np.sqrt(pv), 2, "e4m3").reshape(C * M, D).T).reshape(N, C, M)
    var_term = xv.sum(-1)[:, None, None] + pv.sum(-1)[None, :, :] - 2.0 * cross
    return -(2.0 - 2.0 * dot + LAMDA * var_term)

@@ -1,0 +1,285 @@
+from contextlib import ExitStack
+
+import concourse.mybir as mybir
+from concourse.masks import make_identity
+
+F32 = mybir.dt.float32
+BF16 = mybir.dt.bfloat16
+I32 = mybir.dt.int32
+U32 = mybir.dt.uint32
+U8 = mybir.dt.uint8
+FP8X4 = mybir.dt.float8_e4m3fn_x4
+ALU = mybir.AluOpType
+SQRT = mybir.ActivationFunctionType.Sqrt
+
+LAMDA = 0.00390625
+
+P = 128
+D = 2048
+PROTOS = 4096
+CLASS = 64
+PACK = 4
+PASSES = D // (P * PACK)
+WORDS = D // 2
+PASS_WORDS = WORDS // PASSES
+CHUNK = 256
+ROW_TILES = CHUNK // P
+N_CHUNKS = PROTOS // CHUNK
+CHUNK_CLASSES = CHUNK // CLASS
+
+LEAD = 4
+LAG = 3
+
+FLOPS = 2 * 2 * P * PROTOS * D
+
+
+def tile_probprotoseghead_w_e_kernel(
+    tc, x, x_var, proto_mean_words, proto_mean_scales, proto_var, out
+):
+    nc = tc.nc
+
+    var_rows = proto_var.rearrange("c m d -> (c m) d")
+    out_cols = out.rearrange("n c m -> n (c m)")
+    words_by_pass = (
+        proto_mean_words.rearrange("g p m t -> g p (m t)")
+        .bitcast(I32)
+        .rearrange("(c s) p w -> s p c w", s=PASSES)
+    )
+    scales_by_pass = proto_mean_scales.bitcast(F32).rearrange("(c s) q w -> s q c w", s=PASSES)
+
+    with ExitStack() as stack:
+        stack.enter_context(tc.manual_schedule())
+        keep = stack.enter_context(tc.tile_pool(name="keep", bufs=1))
+        raw_pool = stack.enter_context(tc.tile_pool(name="raw", bufs=LEAD + 1))
+        word_pool = stack.enter_context(tc.tile_pool(name="words", bufs=LAG + 2))
+        grouped_pool = stack.enter_context(tc.tile_pool(name="grouped", bufs=3))
+        code_pool = stack.enter_context(tc.tile_pool(name="codes", bufs=LAG + 1))
+        end_pool = stack.enter_context(tc.tile_pool(name="end", bufs=3))
+        flipped_pool = stack.enter_context(tc.psum_pool(name="flipped", bufs=4))
+        acc_pool = stack.enter_context(tc.psum_pool(name="acc", bufs=2))
+        spread_pool = stack.enter_context(tc.psum_pool(name="spread", bufs=2))
+
+        ident = keep.tile([P, P], F32)
+        make_identity(nc, ident[:])
+
+        mean_scales = keep.tile([P, PROTOS], U8, align_bytes=64)
+        nc.vector.memset(mean_scales[:].bitcast(I32), 0)
+        for s in range(PASSES):
+            for quadrant in range(4):
+                first_row = 32 * quadrant + 4 * s
+                nc.gpsimd.dma_start(
+                    out=mean_scales[first_row : first_row + 4, :]
+                    .bitcast(F32)
+                    .rearrange("r (c w) -> r c w", w=CLASS // 4),
+                    in_=scales_by_pass[s][4 * quadrant : 4 * quadrant + 4],
+                )
+
+        raw = {}
+        mean_words = {}
+        flipped = {}
+        grouped = {}
+        var_codes = {}
+        acc = {}
+        spread = {}
+
+        neg_sp = keep.tile([P, PROTOS // P], F32)
+        scaled = keep.tile([P, D], BF16)
+
+        def sum_row(total, row):
+            nc.vector.tensor_scalar(
+                out=scaled[:], in0=row, scalar1=-LAMDA, scalar2=None,
+                op0=ALU.mult, op1=ALU.add, accum_out=total,
+            )
+
+        def flip(bank, u, column, words):
+            nc.tensor.transpose(bank[:, u, column : column + P], words, ident[:])
+
+        def pairs_in_turn(bank):
+            return bank[:].bitcast(BF16).rearrange("p u (c e) -> p c u e", e=2)
+
+        def load_var(chunk):
+            raw[chunk] = raw_pool.tile([P, ROW_TILES, D], BF16, name="raw")
+            nc.sync.dma_start(
+                out=raw[chunk][:],
+                in_=var_rows[chunk * CHUNK : (chunk + 1) * CHUNK, :].rearrange(
+                    "(r p) d -> p r d", p=P
+                ),
+            )
+
+        def load_words(chunk):
+            mean_words[chunk] = word_pool.tile(
+                [P, PASSES, CHUNK * PACK], U8, name="mean_words", align_bytes=64
+            )
+            classes = slice(chunk * CHUNK_CLASSES, (chunk + 1) * CHUNK_CLASSES)
+            for s in range(PASSES):
+                nc.sync.dma_start(
+                    out=mean_words[chunk][:, s, :].bitcast(I32).rearrange("p (c w) -> p c w", w=CLASS),
+                    in_=words_by_pass[s][:, classes, :],
+                )
+
+        def sum_rows(chunk):
+            for r in range(ROW_TILES):
+                tile_index = chunk * ROW_TILES + r
+                sum_row(neg_sp[:, tile_index : tile_index + 1], raw[chunk][:, r, :])
+
+        def flip_var(chunk, s):
+            flipped[chunk, s] = flipped_pool.tile([P, 2, CHUNK], F32, name="flipped")
+            for u in range(2):
+                first = s * PASS_WORDS + u * P
+                for r in range(ROW_TILES):
+                    words = raw[chunk][:, r, :].bitcast(F32)
+                    flip(flipped[chunk, s], u, r * P, words[:, first : first + P])
+
+        def root_var(chunk, s):
+            if s == 0:
+                grouped[chunk] = grouped_pool.tile(
+                    [P, PASSES, CHUNK, PACK], BF16, name="grouped", align_bytes=64
+                )
+            nc.scalar.activation(
+                out=grouped[chunk][:, s].rearrange("p c (u e) -> p c u e", e=2),
+                in_=pairs_in_turn(flipped[chunk, s]),
+                func=SQRT,
+            )
+
+        def quantise_var(chunk):
+            codes = code_pool.tile([P, PASSES * CHUNK], U32, name="codes", align_bytes=64)
+            plane = code_pool.tile([P, PASSES * CHUNK], U8, name="plane", align_bytes=64)
+            nc.vector.quantize_mx(
+                out=codes[:].bitcast(FP8X4),
+                scales=plane[:],
+                in_=grouped[chunk][:].rearrange("p s c t -> p (s c t)"),
+            )
+            var_codes[chunk] = (codes, plane)
+
+        def multiply(chunk):
+            spread[chunk] = spread_pool.tile([P, CHUNK], F32, name="spread")
+            for r in range(ROW_TILES):
+                tile_index = chunk * ROW_TILES + r
+                nc.tensor.transpose(
+                    spread[chunk][:, r * P : (r + 1) * P],
+                    neg_sp[:, tile_index : tile_index + 1].to_broadcast([P, P]),
+                    ident[:],
+                )
+            acc[chunk] = acc_pool.tile([P, CHUNK], F32, name="acc")
+            codes, plane = var_codes[chunk]
+            columns = slice(chunk * CHUNK, (chunk + 1) * CHUNK)
+            for s in range(PASSES):
+                pixels = slice(s * P, (s + 1) * P)
+                protos = slice(s * CHUNK, (s + 1) * CHUNK)
+                nc.tensor.matmul_mx(
+                    out=acc[chunk][:],
+                    lhsT=xv_codes[:, pixels].bitcast(FP8X4),
+                    lhsT_scale=xv_plane[:, pixels],
+                    rhs=codes[:, protos].bitcast(FP8X4),
+                    rhs_scale=plane[:, protos],
+                    start=(s == 0),
+                    stop=False,
+                )
+            for s in range(PASSES):
+                pixels = slice(s * P, (s + 1) * P)
+                nc.tensor.matmul_mx(
+                    out=acc[chunk][:],
+                    lhsT=x_codes[:, pixels].bitcast(FP8X4),
+                    lhsT_scale=x_plane[:, pixels],
+                    rhs=mean_words[chunk][:, s, :].bitcast(FP8X4),
+                    rhs_scale=mean_scales[4 * s : P, columns],
+                    start=False,
+                    stop=(s == PASSES - 1),
+                )
+
+        def finish(chunk):
+            base = end_pool.tile([P, CHUNK], F32, name="base")
+            nc.vector.tensor_scalar(
+                out=base[:], in0=spread[chunk][:], scalar1=pixel_term[:, 0:1], scalar2=None,
+                op0=ALU.add,
+            )
+            result = end_pool.tile([P, CHUNK], F32, name="result")
+            nc.vector.scalar_tensor_tensor(
+                out=result[:], in0=acc[chunk][:], scalar=2.0, in1=base[:],
+                op0=ALU.mult, op1=ALU.add,
+            )
+            nc.sync.dma_start(
+                out=out_cols[:, chunk * CHUNK : (chunk + 1) * CHUNK], in_=result[:]
+            )
+
+        xv_raw = keep.tile([P, D], BF16)
+        x_raw = keep.tile([P, D], BF16)
+        nc.sync.dma_start(out=xv_raw[:], in_=x_var)
+        nc.sync.dma_start(out=x_raw[:], in_=x)
+        for chunk in range(LEAD):
+            load_var(chunk)
+
+        pixel_term = keep.tile([P, 1], F32)
+        sum_row(pixel_term[:], xv_raw[:])
+        nc.vector.tensor_scalar_add(out=pixel_term[:], in0=pixel_term[:], scalar1=-2.0)
+
+        xv_grouped = keep.tile([P, PASSES * P, PACK], BF16, align_bytes=64)
+        x_grouped = keep.tile([P, PASSES * P, PACK], BF16, align_bytes=64)
+        xv_banks = []
+        x_banks = []
+        for half in range(PASSES // 2):
+            bank = flipped_pool.tile([P, 2, CHUNK], F32, name="flipped")
+            for u in range(2):
+                for i in range(2):
+                    first = (2 * half + i) * PASS_WORDS + u * P
+                    flip(bank, u, i * P, xv_raw[:].bitcast(F32)[:, first : first + P])
+            xv_banks.append(bank)
+        for half in range(PASSES // 2):
+            bank = flipped_pool.tile([P, 2, CHUNK], F32, name="flipped")
+            for u in range(2):
+                for i in range(2):
+                    first = (2 * half + i) * PASS_WORDS
+                    flip(bank, u, i * P, x_raw[:].bitcast(F32)[:, first + u : first + PASS_WORDS : 2])
+            x_banks.append(bank)
+        for half in range(PASSES // 2):
+            columns = slice(half * CHUNK, (half + 1) * CHUNK)
+            nc.scalar.activation(
+                out=xv_grouped[:, columns, :].rearrange("p c (u e) -> p c u e", e=2),
+                in_=pairs_in_turn(xv_banks[half]),
+                func=SQRT,
+                scale=LAMDA * LAMDA,
+            )
+            nc.vector.tensor_copy(
+                out=x_grouped[:, columns, :].rearrange("p c t -> p (c t)").bitcast(F32)
+                .rearrange("p (c u) -> p c u", u=2),
+                in_=x_banks[half][:].rearrange("p u c -> p c u"),
+            )
+
+        x_codes = keep.tile([P, PASSES * P], U32, align_bytes=64)
+        x_plane = keep.tile([P, PASSES * P], U8, align_bytes=64)
+        xv_codes = keep.tile([P, PASSES * P], U32, align_bytes=64)
+        xv_plane = keep.tile([P, PASSES * P], U8, align_bytes=64)
+        nc.vector.quantize_mx(
+            out=x_codes[:].bitcast(FP8X4), scales=x_plane[:],
+            in_=x_grouped[:].rearrange("p c t -> p (c t)"),
+        )
+        nc.vector.quantize_mx(
+            out=xv_codes[:].bitcast(FP8X4), scales=xv_plane[:],
+            in_=xv_grouped[:].rearrange("p c t -> p (c t)"),
+        )
+
+        sum_rows(0)
+        for s in range(PASSES):
+            flip_var(0, s)
+
+        def exists(chunk):
+            return 0 <= chunk < N_CHUNKS
+
+        for step in range(N_CHUNKS + LAG):
+            if exists(step):
+                load_words(step)
+            if exists(step + LEAD):
+                load_var(step + LEAD)
+            if exists(step - LAG):
+                multiply(step - LAG)
+            if exists(step):
+                for s in range(PASSES):
+                    root_var(step, s)
+                    if exists(step + 1):
+                        flip_var(step + 1, s)
+            if exists(step - 1):
+                quantise_var(step - 1)
+            if exists(step + 1):
+                sum_rows(step + 1)
+            if exists(step - LAG):
+                finish(step - LAG)

@@ -45,7 +45,7 @@ def tile_probprotoseghead_w_e_kernel(
         .bitcast(I32)
         .rearrange("(c s) p w -> s p c w", s=PASSES)
     )
-    scales_by_pass = proto_mean_scales.bitcast(F32).rearrange("(c s) q w -> s q c w", s=PASSES)
+    scales_by_pass = proto_mean_scales.bitcast(I32).rearrange("(c s) q w -> s q c w", s=PASSES)
 
     with ExitStack() as stack:
         stack.enter_context(tc.manual_schedule())
@@ -64,15 +64,6 @@ def tile_probprotoseghead_w_e_kernel(
 
         mean_scales = keep.tile([P, PROTOS], U8, align_bytes=64)
         nc.vector.memset(mean_scales[:].bitcast(I32), 0)
-        for s in range(PASSES):
-            for quadrant in range(4):
-                first_row = 32 * quadrant + 4 * s
-                nc.gpsimd.dma_start(
-                    out=mean_scales[first_row : first_row + 4, :]
-                    .bitcast(F32)
-                    .rearrange("r (c w) -> r c w", w=CLASS // 4),
-                    in_=scales_by_pass[s][4 * quadrant : 4 * quadrant + 4],
-                )
 
         raw = {}
         mean_words = {}
@@ -208,6 +199,15 @@ def tile_probprotoseghead_w_e_kernel(
         nc.sync.dma_start(out=x_raw[:], in_=x)
         for chunk in range(LEAD):
             load_var(chunk)
+        for s in range(PASSES):
+            for quadrant in range(4):
+                first_row = 32 * quadrant + 4 * s
+                nc.sync.dma_start(
+                    out=mean_scales[first_row : first_row + 4, :]
+                    .bitcast(I32)
+                    .rearrange("r (c w) -> r c w", w=CLASS // 4),
+                    in_=scales_by_pass[s][4 * quadrant : 4 * quadrant + 4],
+                )
 
         pixel_term = keep.tile([P, 1], F32)
         sum_row(pixel_term[:], xv_raw[:])

@@ -18,6 +18,7 @@ P = 128
 D = 2048
 PROTOS = 4096
 CLASS = 64
+N_CLASSES = PROTOS // CLASS
 PACK = 4
 PASSES = D // (P * PACK)
 WORDS = D // 2
@@ -45,7 +46,6 @@ def tile_probprotoseghead_w_e_kernel(
         .bitcast(I32)
         .rearrange("(c s) p w -> s p c w", s=PASSES)
     )
-    scales_by_pass = proto_mean_scales.bitcast(I32).rearrange("(c s) q w -> s q c w", s=PASSES)
 
     with ExitStack() as stack:
         stack.enter_context(tc.manual_schedule())
@@ -64,6 +64,24 @@ def tile_probprotoseghead_w_e_kernel(
 
         mean_scales = keep.tile([P, PROTOS], U8, align_bytes=64)
         nc.vector.memset(mean_scales[:].bitcast(I32), 0)
+
+        def load_scales(queue, word, first_class, end_class):
+            scales_by_pass = proto_mean_scales.bitcast(word).rearrange(
+                "(c s) q w -> s q c w", s=PASSES
+            )
+            classes = slice(first_class, end_class)
+            columns = slice(first_class * CLASS, end_class * CLASS)
+            for s in range(PASSES):
+                for quadrant in range(4):
+                    first_row = 32 * quadrant + 4 * s
+                    queue.dma_start(
+                        out=mean_scales[first_row : first_row + 4, columns]
+                        .bitcast(word)
+                        .rearrange("r (c w) -> r c w", w=CLASS // 4),
+                        in_=scales_by_pass[s][4 * quadrant : 4 * quadrant + 4, classes, :],
+                    )
+
+        load_scales(nc.gpsimd, F32, N_CLASSES // 2, N_CLASSES)
 
         raw = {}
         mean_words = {}
@@ -199,15 +217,7 @@ def tile_probprotoseghead_w_e_kernel(
         nc.sync.dma_start(out=x_raw[:], in_=x)
         for chunk in range(LEAD):
             load_var(chunk)
-        for s in range(PASSES):
-            for quadrant in range(4):
-                first_row = 32 * quadrant + 4 * s
-                nc.sync.dma_start(
-                    out=mean_scales[first_row : first_row + 4, :]
-                    .bitcast(I32)
-                    .rearrange("r (c w) -> r c w", w=CLASS // 4),
-                    in_=scales_by_pass[s][4 * quadrant : 4 * quadrant + 4],
-                )
+        load_scales(nc.sync, I32, 0, N_CLASSES // 2)
 
         pixel_term = keep.tile([P, 1], F32)
         sum_row(pixel_term[:], xv_raw[:])

from contextlib import ExitStack

import concourse.mybir as mybir
from concourse.masks import make_identity

F32 = mybir.dt.float32
BF16 = mybir.dt.bfloat16
I32 = mybir.dt.int32
U32 = mybir.dt.uint32
U8 = mybir.dt.uint8
FP8X4 = mybir.dt.float8_e4m3fn_x4
ALU = mybir.AluOpType
SQRT = mybir.ActivationFunctionType.Sqrt

LAMDA = 0.00390625

P = 128
D = 2048
PROTOS = 4096
CLASS = 64
N_CLASSES = PROTOS // CLASS
PACK = 4
PASSES = D // (P * PACK)
WORDS = D // 2
PASS_WORDS = WORDS // PASSES
CHUNK = 256
ROW_TILES = CHUNK // P
N_CHUNKS = PROTOS // CHUNK
CHUNK_CLASSES = CHUNK // CLASS

LEAD = 4
LAG = 3

FLOPS = 2 * 2 * P * PROTOS * D


def tile_probprotoseghead_w_e_kernel(
    tc, x, x_var, proto_mean_words, proto_mean_scales, proto_var, out
):
    nc = tc.nc

    var_rows = proto_var.rearrange("c m d -> (c m) d")
    out_cols = out.rearrange("n c m -> n (c m)")
    words_by_pass = (
        proto_mean_words.rearrange("g p m t -> g p (m t)")
        .bitcast(I32)
        .rearrange("(c s) p w -> s p c w", s=PASSES)
    )

    with ExitStack() as stack:
        stack.enter_context(tc.manual_schedule())
        keep = stack.enter_context(tc.tile_pool(name="keep", bufs=1))
        raw_pool = stack.enter_context(tc.tile_pool(name="raw", bufs=LEAD + 1))
        word_pool = stack.enter_context(tc.tile_pool(name="words", bufs=LAG + 2))
        grouped_pool = stack.enter_context(tc.tile_pool(name="grouped", bufs=3))
        code_pool = stack.enter_context(tc.tile_pool(name="codes", bufs=LAG + 1))
        end_pool = stack.enter_context(tc.tile_pool(name="end", bufs=3))
        flipped_pool = stack.enter_context(tc.psum_pool(name="flipped", bufs=4))
        acc_pool = stack.enter_context(tc.psum_pool(name="acc", bufs=2))
        spread_pool = stack.enter_context(tc.psum_pool(name="spread", bufs=2))

        ident = keep.tile([P, P], F32)
        make_identity(nc, ident[:])

        mean_scales = keep.tile([P, PROTOS], U8, align_bytes=64)
        nc.vector.memset(mean_scales[:].bitcast(I32), 0)

        def load_scales(queue, word, first_class, end_class):
            scales_by_pass = proto_mean_scales.bitcast(word).rearrange(
                "(c s) q w -> s q c w", s=PASSES
            )
            classes = slice(first_class, end_class)
            columns = slice(first_class * CLASS, end_class * CLASS)
            for s in range(PASSES):
                for quadrant in range(4):
                    first_row = 32 * quadrant + 4 * s
                    queue.dma_start(
                        out=mean_scales[first_row : first_row + 4, columns]
                        .bitcast(word)
                        .rearrange("r (c w) -> r c w", w=CLASS // 4),
                        in_=scales_by_pass[s][4 * quadrant : 4 * quadrant + 4, classes, :],
                    )

        load_scales(nc.gpsimd, F32, N_CLASSES // 2, N_CLASSES)

        raw = {}
        mean_words = {}
        flipped = {}
        grouped = {}
        var_codes = {}
        acc = {}
        spread = {}

        neg_sp = keep.tile([P, PROTOS // P], F32)
        scaled = keep.tile([P, D], BF16)

        def sum_row(total, row):
            nc.vector.tensor_scalar(
                out=scaled[:], in0=row, scalar1=-LAMDA, scalar2=None,
                op0=ALU.mult, op1=ALU.add, accum_out=total,
            )

        def flip(bank, u, column, words):
            nc.tensor.transpose(bank[:, u, column : column + P], words, ident[:])

        def pairs_in_turn(bank):
            return bank[:].bitcast(BF16).rearrange("p u (c e) -> p c u e", e=2)

        def load_var(chunk):
            raw[chunk] = raw_pool.tile([P, ROW_TILES, D], BF16, name="raw")
            nc.sync.dma_start(
                out=raw[chunk][:],
                in_=var_rows[chunk * CHUNK : (chunk + 1) * CHUNK, :].rearrange(
                    "(r p) d -> p r d", p=P
                ),
            )

        def load_words(chunk):
            mean_words[chunk] = word_pool.tile(
                [P, PASSES, CHUNK * PACK], U8, name="mean_words", align_bytes=64
            )
            classes = slice(chunk * CHUNK_CLASSES, (chunk + 1) * CHUNK_CLASSES)
            for s in range(PASSES):
                nc.sync.dma_start(
                    out=mean_words[chunk][:, s, :].bitcast(I32).rearrange("p (c w) -> p c w", w=CLASS),
                    in_=words_by_pass[s][:, classes, :],
                )

        def sum_rows(chunk):
            for r in range(ROW_TILES):
                tile_index = chunk * ROW_TILES + r
                sum_row(neg_sp[:, tile_index : tile_index + 1], raw[chunk][:, r, :])

        def flip_var(chunk, s):
            flipped[chunk, s] = flipped_pool.tile([P, 2, CHUNK], F32, name="flipped")
            for u in range(2):
                first = s * PASS_WORDS + u * P
                for r in range(ROW_TILES):
                    words = raw[chunk][:, r, :].bitcast(F32)
                    flip(flipped[chunk, s], u, r * P, words[:, first : first + P])

        def root_var(chunk, s):
            if s == 0:
                grouped[chunk] = grouped_pool.tile(
                    [P, PASSES, CHUNK, PACK], BF16, name="grouped", align_bytes=64
                )
            nc.scalar.activation(
                out=grouped[chunk][:, s].rearrange("p c (u e) -> p c u e", e=2),
                in_=pairs_in_turn(flipped[chunk, s]),
                func=SQRT,
            )

        def quantise_var(chunk):
            codes = code_pool.tile([P, PASSES * CHUNK], U32, name="codes", align_bytes=64)
            plane = code_pool.tile([P, PASSES * CHUNK], U8, name="plane", align_bytes=64)
            nc.vector.quantize_mx(
                out=codes[:].bitcast(FP8X4),
                scales=plane[:],
                in_=grouped[chunk][:].rearrange("p s c t -> p (s c t)"),
            )
            var_codes[chunk] = (codes, plane)

        def multiply(chunk):
            spread[chunk] = spread_pool.tile([P, CHUNK], F32, name="spread")
            for r in range(ROW_TILES):
                tile_index = chunk * ROW_TILES + r
                nc.tensor.transpose(
                    spread[chunk][:, r * P : (r + 1) * P],
                    neg_sp[:, tile_index : tile_index + 1].to_broadcast([P, P]),
                    ident[:],
                )
            acc[chunk] = acc_pool.tile([P, CHUNK], F32, name="acc")
            codes, plane = var_codes[chunk]
            columns = slice(chunk * CHUNK, (chunk + 1) * CHUNK)
            for s in range(PASSES):
                pixels = slice(s * P, (s + 1) * P)
                protos = slice(s * CHUNK, (s + 1) * CHUNK)
                nc.tensor.matmul_mx(
                    out=acc[chunk][:],
                    lhsT=xv_codes[:, pixels].bitcast(FP8X4),
                    lhsT_scale=xv_plane[:, pixels],
                    rhs=codes[:, protos].bitcast(FP8X4),
                    rhs_scale=plane[:, protos],
                    start=(s == 0),
                    stop=False,
                )
            for s in range(PASSES):
                pixels = slice(s * P, (s + 1) * P)
                nc.tensor.matmul_mx(
                    out=acc[chunk][:],
                    lhsT=x_codes[:, pixels].bitcast(FP8X4),
                    lhsT_scale=x_plane[:, pixels],
                    rhs=mean_words[chunk][:, s, :].bitcast(FP8X4),
                    rhs_scale=mean_scales[4 * s : P, columns],
                    start=False,
                    stop=(s == PASSES - 1),
                )

        def finish(chunk):
            base = end_pool.tile([P, CHUNK], F32, name="base")
            nc.vector.tensor_scalar(
                out=base[:], in0=spread[chunk][:], scalar1=pixel_term[:, 0:1], scalar2=None,
                op0=ALU.add,
            )
            result = end_pool.tile([P, CHUNK], F32, name="result")
            nc.vector.scalar_tensor_tensor(
                out=result[:], in0=acc[chunk][:], scalar=2.0, in1=base[:],
                op0=ALU.mult, op1=ALU.add,
            )
            nc.sync.dma_start(
                out=out_cols[:, chunk * CHUNK : (chunk + 1) * CHUNK], in_=result[:]
            )

        xv_raw = keep.tile([P, D], BF16)
        x_raw = keep.tile([P, D], BF16)
        nc.sync.dma_start(out=xv_raw[:], in_=x_var)
        nc.sync.dma_start(out=x_raw[:], in_=x)
        for chunk in range(LEAD):
            load_var(chunk)
        load_scales(nc.sync, I32, 0, N_CLASSES // 2)

        pixel_term = keep.tile([P, 1], F32)
        sum_row(pixel_term[:], xv_raw[:])
        nc.vector.tensor_scalar_add(out=pixel_term[:], in0=pixel_term[:], scalar1=-2.0)

        xv_grouped = keep.tile([P, PASSES * P, PACK], BF16, align_bytes=64)
        x_grouped = keep.tile([P, PASSES * P, PACK], BF16, align_bytes=64)
        xv_banks = []
        x_banks = []
        for half in range(PASSES // 2):
            bank = flipped_pool.tile([P, 2, CHUNK], F32, name="flipped")
            for u in range(2):
                for i in range(2):
                    first = (2 * half + i) * PASS_WORDS + u * P
                    flip(bank, u, i * P, xv_raw[:].bitcast(F32)[:, first : first + P])
            xv_banks.append(bank)
        for half in range(PASSES // 2):
            bank = flipped_pool.tile([P, 2, CHUNK], F32, name="flipped")
            for u in range(2):
                for i in range(2):
                    first = (2 * half + i) * PASS_WORDS
                    flip(bank, u, i * P, x_raw[:].bitcast(F32)[:, first + u : first + PASS_WORDS : 2])
            x_banks.append(bank)
        for half in range(PASSES // 2):
            columns = slice(half * CHUNK, (half + 1) * CHUNK)
            nc.scalar.activation(
                out=xv_grouped[:, columns, :].rearrange("p c (u e) -> p c u e", e=2),
                in_=pairs_in_turn(xv_banks[half]),
                func=SQRT,
                scale=LAMDA * LAMDA,
            )
            nc.vector.tensor_copy(
                out=x_grouped[:, columns, :].rearrange("p c t -> p (c t)").bitcast(F32)
                .rearrange("p (c u) -> p c u", u=2),
                in_=x_banks[half][:].rearrange("p u c -> p c u"),
            )

        x_codes = keep.tile([P, PASSES * P], U32, align_bytes=64)
        x_plane = keep.tile([P, PASSES * P], U8, align_bytes=64)
        xv_codes = keep.tile([P, PASSES * P], U32, align_bytes=64)
        xv_plane = keep.tile([P, PASSES * P], U8, align_bytes=64)
        nc.vector.quantize_mx(
            out=x_codes[:].bitcast(FP8X4), scales=x_plane[:],
            in_=x_grouped[:].rearrange("p c t -> p (c t)"),
        )
        nc.vector.quantize_mx(
            out=xv_codes[:].bitcast(FP8X4), scales=xv_plane[:],
            in_=xv_grouped[:].rearrange("p c t -> p (c t)"),
        )

        sum_rows(0)
        for s in range(PASSES):
            flip_var(0, s)

        def exists(chunk):
            return 0 <= chunk < N_CHUNKS

        for step in range(N_CHUNKS + LAG):
            if exists(step):
                load_words(step)
            if exists(step + LEAD):
                load_var(step + LEAD)
            if exists(step - LAG):
                multiply(step - LAG)
            if exists(step):
                for s in range(PASSES):
                    root_var(step, s)
                    if exists(step + 1):
                        flip_var(step + 1, s)
            if exists(step - 1):
                quantise_var(step - 1)
            if exists(step + 1):
                sum_rows(step + 1)
            if exists(step - LAG):
                finish(step - LAG)
